import numpy as np
import ml_dtypes


def mxq(x, axis, fmt="e4m3"):
    dtype, down = {"e4m3": (ml_dtypes.float8_e4m3fn, 7), "e5m2": (ml_dtypes.float8_e5m2, 14)}[fmt]
    v = np.moveaxis(np.asarray(x, np.float32).astype(ml_dtypes.bfloat16).astype(np.float64), axis, -1)
    blocks = v.reshape(v.shape[:-1] + (-1, 32))
    amax = np.abs(blocks).max(-1, keepdims=True)
    byte = np.maximum(np.where(amax > 0, np.frexp(amax)[1] - 1 + 127, 0) - down, 1)
    scale = np.exp2(byte - 127.0)
    codes = (blocks / scale).astype(np.float32).astype(dtype).astype(np.float64)
    return np.moveaxis((codes * scale).reshape(v.shape), -1, axis)


WIDE = False


def mx_kscale(k):
    if not WIDE:
        return np.ones(k)
    levels = np.array([10, -10, 5, -5, 0])
    if k % 512:
        return np.exp2(np.random.permutation(np.resize(levels, k // 32))).repeat(32)
    a = np.empty((k // 512, 16))
    for p in range(k // 512):
        a[p, :8] = np.random.permutation(np.resize(levels, 8))
        for g in range(8):
            far = levels[np.abs(levels - a[p, g]) >= 10]
            a[p, g + 8] = far[np.random.randint(len(far))]
    return np.exp2(a.ravel()).repeat(32)


BF16 = ml_dtypes.bfloat16


def bf(x):
    return np.asarray(x, np.float32).astype(BF16)


def f64(x):
    return np.asarray(x).astype(np.float64)


Nc, Ns, Nt, d_h, BS = 64, 8, 16, 128, 64
I, J = Ns * Nt, Nc * Nt


def setup_inputs():
    s = mx_kscale(J)
    Ac = (np.random.random((Ns, Nc)) < 3.2 / Ns).astype(np.float64)
    Ac[np.random.randint(0, Ns, Nc), np.arange(Nc)] = 1.0
    Ac[np.arange(Ns), np.random.randint(0, Nc, Ns)] = 1.0
    As = (np.random.random((Ns, Ns)) < 0.05).astype(np.float64)
    AA = np.dot(np.dot(As, As), Ac) + np.dot(As, Ac) + Ac
    AA = (AA != 0).astype(np.float64)
    AA_mask = np.tile(AA, (Nt, Nt))
    g = 1.0 / np.sqrt(0.5 * J * AA.mean())
    GCW = np.random.standard_normal((I, J)) * g * s[None, :]
    GCB = np.random.standard_normal((I, d_h)) * 0.5
    h = np.random.standard_normal((BS, Nc, Nt, d_h)) / s.reshape(Nt, Nc).T[None, :, :, None]
    e = np.random.standard_normal(1) * 0.1
    return {"h": bf(h), "e": bf(e), "AA_mask": bf(AA_mask), "GCW": bf(GCW), "GCB": bf(GCB)}


def reference(h, e, AA_mask, GCW, GCB):
    bs = h.shape[0]
    A = np.maximum(f64(AA_mask) * f64(GCW), 0.0)
    x = np.transpose(f64(h), (0, 2, 1, 3)).reshape(bs, Nt * Nc, d_h)
    x = np.maximum((mxq(A, 1, "e4m3") @ mxq(x, 1, "e4m3")) + f64(GCB), 0.0)
    x = x.reshape(bs, Nt, Ns, d_h)
    x = np.transpose(x, (0, 2, 1, 3))
    return x

@@ -1,0 +1,252 @@
+from contextlib import ExitStack
+
+import concourse.mybir as mybir
+from concourse.masks import make_identity
+
+BF16 = mybir.dt.bfloat16
+F32 = mybir.dt.float32
+U32 = mybir.dt.uint32
+U8 = mybir.dt.uint8
+I32 = mybir.dt.int32
+FP8X4 = mybir.dt.float8_e4m3fn_x4
+ALU = mybir.AluOpType
+ACT = mybir.ActivationFunctionType
+
+P = 128
+FLOPS = 2 * 64 * 128 * 1024 * 128
+UNITS = [(0, 1), (1, 1), (2, 2), (4, 2), (6, 2), (8, 2), (10, 2), (12, 2), (14, 1), (15, 1)]
+
+
+def tile_gcnfast_t_kernel(tc, h, e, AA_mask, GCW, GCB, out):
+    nc = tc.nc
+    nu = len(UNITS)
+    with ExitStack() as ctx:
+        ctx.enter_context(tc.manual_schedule())
+        const = ctx.enter_context(tc.tile_pool(name="const", bufs=1))
+        rawp = ctx.enter_context(tc.tile_pool(name="rawp", bufs=1))
+        grpp = ctx.enter_context(tc.tile_pool(name="grpp", bufs=4))
+        codp = ctx.enter_context(tc.tile_pool(name="codp", bufs=5))
+        yp = ctx.enter_context(tc.tile_pool(name="yp", bufs=3))
+        psa = ctx.enter_context(tc.psum_pool(name="psa", bufs=8))
+
+        hv = h.rearrange("b (c j) (u t) d -> u (b c) j (t d)", j=4, u=2)
+        ov = out.rearrange("b s t d -> (s t) b d")
+
+        ident = const.tile([P, P], F32, name="ident")
+        perm = const.tile([P, P], F32, name="perm")
+        permb = const.tile([P, P], BF16, name="permb")
+        gcw = const.tile([P, 1024], BF16, name="gcw")
+        msk = const.tile([P, 1024], BF16, name="msk")
+        pm = const.tile([P, 1024], BF16, name="pm")
+        gcb = const.tile([P, P], BF16, name="gcb")
+        bias = const.tile([P, P], F32, name="bias")
+        cd = const.tile([P, 1024], U32, name="cd", align_bytes=64)
+        sd = const.tile([P, 1024], U8, name="sd", align_bytes=64)
+        a_codes = const.tile([P, 4096], U32, name="a_codes", align_bytes=64)
+        raw = rawp.tile([P, 16, 4, 8, P], BF16, name="raw")
+
+        grp = {}
+        acc = {}
+        codes = {}
+        ys = {}
+
+        def load(g, u, a, b):
+            eng = nc.sync if u == 0 else nc.scalar
+            eng.dma_start(
+                out=raw[64 * u : 64 * u + 64, g, :, a:b, :].rearrange("p j t d -> p j (t d)"),
+                in_=hv[u, 64 * g : 64 * g + 64, :, P * a : P * b],
+            )
+
+        def load_group(g):
+            load(g, 0, 0, 8)
+            load(g, 1, 0, 8)
+
+        def views(u, c, s):
+            g0, n = UNITS[u]
+            if (u, c) not in grp:
+                grp[(u, c)] = grpp.tile([P, 4096], BF16, name="grp", tag="grp", align_bytes=64)
+            src = raw[:, g0 + s, :, 4 * c : 4 * c + 4, :].rearrange("p j t (c i) -> p t c j i", i=4)
+            dst = grp[(u, c)][:, 0 : 2048 * n].rearrange("p (t s c i j) -> p s t c j i", t=4, s=n, c=32, i=4, j=4)
+            return src, dst[:, s]
+
+        def regroup_v(u, c, s, a, b):
+            src, dst = views(u, c, s)
+            if b - a == 1:
+                nc.vector.tensor_copy(out=dst[:, a], in_=src[:, a])
+            elif b > a:
+                nc.vector.tensor_copy(out=dst[:, a:b], in_=src[:, a:b])
+
+        def regroup_s(u, c, s, a, b):
+            src, dst = views(u, c, s)
+            if b - a == 1:
+                nc.scalar.copy(out=dst[:, a], in_=src[:, a])
+            elif b > a:
+                nc.scalar.copy(out=dst[:, a:b], in_=src[:, a:b])
+
+        def regroup(u, c):
+            n = UNITS[u][1]
+            if n == 2:
+                regroup_s(u, c, 0, 0, 4)
+                if c == 1:
+                    regroup_s(u, c, 1, 0, 1)
+                    regroup_v(u, c, 1, 1, 2)
+                    regroup_v(u, c, 1, 2, 4)
+                else:
+                    regroup_v(u, c, 1, 0, 4)
+            else:
+                regroup_s(u, c, 0, 0, 2)
+                regroup_v(u, c, 0, 2, 4)
+
+        def quant(u, c):
+            w = P * UNITS[u][1]
+            cod = codp.tile([P, 1024], U32, name="cod", tag="cod", align_bytes=64)
+            scl = codp.tile([P, 1024], U8, name="scl", tag="scl", align_bytes=64)
+            nc.vector.quantize_mx(
+                out=cod[:, 0 : 4 * w].bitcast(FP8X4), scales=scl[:, 0 : 4 * w], in_=grp[(u, c)][:, 0 : 16 * w]
+            )
+            codes[(u, c)] = (cod, scl)
+
+        def mm(u, b, tr):
+            w = P * UNITS[u][1]
+            per_bank = 1 if u == nu - 1 else 512 // w
+            k, lo = b // per_bank, (b % per_bank) * w
+            if (u, k) not in acc:
+                acc[(u, k)] = psa.tile([P, 512], F32, name="acc", tag="acc")
+            cod, scl = codes[(u, tr // 4)]
+            col = 1024 * b + P * tr
+            t = tr % 4
+            nc.tensor.matmul_mx(
+                out=acc[(u, k)][:, lo : lo + w],
+                lhsT=a_codes[:, col : col + P].bitcast(FP8X4),
+                lhsT_scale=sd[:, P * tr : P * tr + P],
+                rhs=cod[:, w * t : w * t + w].bitcast(FP8X4),
+                rhs_scale=scl[:, w * t : w * t + w],
+                start=(tr == 0),
+                stop=(tr == 7),
+            )
+
+        def mm_unit(u):
+            for b in range(4):
+                for tr in range(8):
+                    mm(u, b, tr)
+
+        def add(u):
+            n = UNITS[u][1]
+            w = P * n
+            per_bank = 1 if u == nu - 1 else 512 // w
+            ys[u] = yp.tile([P, n, 4, P], F32, name="y", tag="y")
+            for k in range(4 // per_bank):
+                nc.vector.tensor_tensor(
+                    out=ys[u][:, :, per_bank * k : per_bank * (k + 1), :].rearrange("p s b d -> p b s d"),
+                    in0=acc[(u, k)][:, 0 : per_bank * w].rearrange("p (b s d) -> p b s d", b=per_bank, s=n),
+                    in1=bias[:].unsqueeze(1).unsqueeze(1).to_broadcast([P, per_bank, n, P]),
+                    op=ALU.add,
+                )
+
+        def relu(u):
+            yf = ys[u][:].rearrange("p s b d -> p (s b d)")
+            nc.scalar.activation(out=yf, in_=yf, func=ACT.Relu)
+
+        def store(u):
+            g0, n = UNITS[u]
+            nc.sync.dma_start(
+                out=ov[:, 4 * g0 : 4 * (g0 + n), :], in_=ys[u][:].rearrange("p s b d -> p (s b) d")
+            )
+
+        warm = const.tile([P, 16], F32, name="warm")
+        nc.gpsimd.memset(warm[:], 0.0)
+        make_identity(nc, ident[:])
+        nc.gpsimd.memset(a_codes[:, 0:2048].bitcast(I32), 0)
+        nc.vector.memset(a_codes[:, 2048:4096].bitcast(I32), 0)
+        nc.sync.dma_start(out=gcw[:], in_=GCW)
+        nc.sync.dma_start(out=msk[:], in_=AA_mask)
+        load(0, 0, 0, 4)
+        load(0, 1, 0, 4)
+        load(0, 0, 4, 8)
+        load(0, 1, 4, 8)
+        load_group(1)
+        nc.scalar.activation(out=warm[:], in_=warm[:], func=ACT.Relu)
+        nc.sync.dma_start(out=gcb[:], in_=GCB)
+        load_group(2)
+        nc.vector.tensor_copy(
+            out=perm[:].rearrange("p (s t) -> p s t", s=8), in_=ident[:].rearrange("p (t s) -> p s t", s=8)
+        )
+        nc.vector.scalar_tensor_tensor(out=pm[:], in0=gcw[:], scalar=0.0, in1=msk[:], op0=ALU.max, op1=ALU.mult)
+
+        pa = grpp.tile([P, 4096], BF16, name="pa", tag="grp", align_bytes=64)
+        gd = grpp.tile([P, 4096], BF16, name="gd", tag="grp", align_bytes=64)
+        paw = pa[:].bitcast(F32)
+        gdw = gd[:].bitcast(F32)
+        pav = paw.rearrange("p (t w u b c) -> p w u t b c", t=8, w=2, u=2, b=4, c=16)
+        pmv = pm[:].bitcast(F32).rearrange("p (u t c w) -> p w u t c", u=2, t=8, c=16, w=2)
+        for w in range(2):
+            for u in range(2):
+                dst = pav[:, w, u]
+                src = pmv[:, w, u].unsqueeze(2).to_broadcast([P, 8, 4, 16])
+                if u == 0:
+                    nc.vector.tensor_copy(out=dst, in_=src)
+                else:
+                    nc.scalar.copy(out=dst, in_=src)
+        nc.vector.tensor_copy(out=permb[:], in_=perm[:])
+        banks = []
+        for k in range(4):
+            bank = psa.tile([P, 2, 2, P], F32, name="at", tag="acc")
+            for t in range(2):
+                for w in range(2):
+                    lo = (2 * k + t) * 256 + w * P
+                    nc.tensor.transpose(out=bank[:, t, w, :], in_=paw[:, lo : lo + P], identity=perm[:])
+            banks.append(bank)
+        bps = psa.tile([P, 512], F32, name="bps", tag="acc")
+        nc.tensor.matmul(out=bps[:, 0:P], lhsT=permb[:], rhs=gcb[:], start=True, stop=True)
+        regroup(0, 0)
+        for k in range(4):
+            dst = gdw[:, 512 * k : 512 * k + 512].rearrange("p (t m w) -> p t m w", t=2, m=P, w=2)
+            src = banks[k][:].rearrange("p t w m -> p t m w")
+            if k % 2 == 0:
+                nc.vector.tensor_copy(out=dst, in_=src)
+            else:
+                nc.scalar.copy(out=dst, in_=src)
+        load_group(3)
+        nc.vector.quantize_mx(out=cd[:].bitcast(FP8X4), scales=sd[:], in_=gd[:])
+        for u in range(2):
+            for b in range(4):
+                lo = 64 * u + 16 * b
+                nc.sync.dma_start(
+                    out=a_codes[lo : lo + 16, 1024 * b : 1024 * b + 1024].bitcast(I32),
+                    in_=cd[lo : lo + 16, :].bitcast(I32),
+                )
+        nc.vector.tensor_copy(out=bias[:], in_=bps[:, 0:P])
+        regroup(0, 1)
+        quant(0, 0)
+
+        for u in range(1, nu):
+            g0, n = UNITS[u]
+            for g in range(g0 + 3, g0 + 3 + n):
+                if g < 16:
+                    load_group(g)
+            regroup(u, 0)
+            quant(u - 1, 1)
+            mm_unit(u - 1)
+            if u >= 3:
+                relu(u - 3)
+                store(u - 3)
+            regroup(u, 1)
+            if u >= 2:
+                add(u - 2)
+            quant(u, 0)
+
+        for tr in range(4):
+            for b in range(4):
+                mm(nu - 1, b, tr)
+        relu(nu - 3)
+        store(nu - 3)
+        quant(nu - 1, 1)
+        add(nu - 2)
+        relu(nu - 2)
+        store(nu - 2)
+        for tr in range(4, 8):
+            for b in range(4):
+                mm(nu - 1, b, tr)
+        add(nu - 1)
+        relu(nu - 1)
+        store(nu - 1)

@@ -7,14 +7,13 @@ BF16 = mybir.dt.bfloat16
 F32 = mybir.dt.float32
 U32 = mybir.dt.uint32
 U8 = mybir.dt.uint8
-I32 = mybir.dt.int32
 FP8X4 = mybir.dt.float8_e4m3fn_x4
 ALU = mybir.AluOpType
 ACT = mybir.ActivationFunctionType
 
 P = 128
 FLOPS = 2 * 64 * 128 * 1024 * 128
-UNITS = [(0, 1), (1, 1), (2, 2), (4, 2), (6, 2), (8, 2), (10, 2), (12, 2), (14, 1), (15, 1)]
+UNITS = [(a, 4) for a in range(0, 60, 4)] + [(60, 2), (62, 2)]
 
 
 def tile_gcnfast_t_kernel(tc, h, e, AA_mask, GCW, GCB, out):
@@ -25,11 +24,11 @@ def tile_gcnfast_t_kernel(tc, h, e, AA_mask, GCW, GCB, out):
         const = ctx.enter_context(tc.tile_pool(name="const", bufs=1))
         rawp = ctx.enter_context(tc.tile_pool(name="rawp", bufs=1))
         grpp = ctx.enter_context(tc.tile_pool(name="grpp", bufs=4))
-        codp = ctx.enter_context(tc.tile_pool(name="codp", bufs=5))
-        yp = ctx.enter_context(tc.tile_pool(name="yp", bufs=3))
+        codp = ctx.enter_context(tc.tile_pool(name="codp", bufs=4))
+        yp = ctx.enter_context(tc.tile_pool(name="yp", bufs=6))
         psa = ctx.enter_context(tc.psum_pool(name="psa", bufs=8))
 
-        hv = h.rearrange("b (c j) (u t) d -> u (b c) j (t d)", j=4, u=2)
+        hv = h.rearrange("b (x c) t d -> b x t c d", x=2)
         ov = out.rearrange("b s t d -> (s t) b d")
 
         ident = const.tile([P, P], F32, name="ident")
@@ -37,216 +36,139 @@ def tile_gcnfast_t_kernel(tc, h, e, AA_mask, GCW, GCB, out):
         permb = const.tile([P, P], BF16, name="permb")
         gcw = const.tile([P, 1024], BF16, name="gcw")
         msk = const.tile([P, 1024], BF16, name="msk")
+        am = const.tile([P, 1024], BF16, name="am")
         pm = const.tile([P, 1024], BF16, name="pm")
         gcb = const.tile([P, P], BF16, name="gcb")
         bias = const.tile([P, P], F32, name="bias")
-        cd = const.tile([P, 1024], U32, name="cd", align_bytes=64)
-        sd = const.tile([P, 1024], U8, name="sd", align_bytes=64)
-        a_codes = const.tile([P, 4096], U32, name="a_codes", align_bytes=64)
-        raw = rawp.tile([P, 16, 4, 8, P], BF16, name="raw")
+        warm = const.tile([P, 16], F32, name="warm")
+        gd = const.tile([P, 1024], BF16, name="gd", align_bytes=64)
+        a_codes = const.tile([P, 256], U32, name="a_codes", align_bytes=64)
+        a_scl = const.tile([P, 256], U8, name="a_scl", align_bytes=64)
+        raw = rawp.tile([P, 64, 2, 4, P], BF16, name="raw")
 
         grp = {}
         acc = {}
         codes = {}
         ys = {}
 
-        def load(g, u, a, b):
-            eng = nc.sync if u == 0 else nc.scalar
-            eng.dma_start(
-                out=raw[64 * u : 64 * u + 64, g, :, a:b, :].rearrange("p j t d -> p j (t d)"),
-                in_=hv[u, 64 * g : 64 * g + 64, :, P * a : P * b],
-            )
+        def load(b):
+            for x in range(2):
+                nc.sync.dma_start(out=raw[:, b, x, :, :], in_=hv[b, x])
 
-        def load_group(g):
-            load(g, 0, 0, 8)
-            load(g, 1, 0, 8)
+        def views(u, x):
+            b0, n = UNITS[u]
+            if u not in grp:
+                grp[u] = grpp.tile([P, 4096], BF16, name="grp", tag="grp", align_bytes=64)
+            src = raw[:, b0 : b0 + n, x, :, :].rearrange("p b j (c i) -> p b c j i", i=4)
+            dst = grp[u][:, 512 * n * x : 512 * n * (x + 1)].rearrange("p (b c i j) -> p b c j i", b=n, c=32, i=4, j=4)
+            return src, dst
 
-        def views(u, c, s):
-            g0, n = UNITS[u]
-            if (u, c) not in grp:
-                grp[(u, c)] = grpp.tile([P, 4096], BF16, name="grp", tag="grp", align_bytes=64)
-            src = raw[:, g0 + s, :, 4 * c : 4 * c + 4, :].rearrange("p j t (c i) -> p t c j i", i=4)
-            dst = grp[(u, c)][:, 0 : 2048 * n].rearrange("p (t s c i j) -> p s t c j i", t=4, s=n, c=32, i=4, j=4)
-            return src, dst[:, s]
-
-        def regroup_v(u, c, s, a, b):
-            src, dst = views(u, c, s)
+        def regroup(u, x, a, b, op):
+            src, dst = views(u, x)
             if b - a == 1:
-                nc.vector.tensor_copy(out=dst[:, a], in_=src[:, a])
+                op(out=dst[:, a], in_=src[:, a])
             elif b > a:
-                nc.vector.tensor_copy(out=dst[:, a:b], in_=src[:, a:b])
+                op(out=dst[:, a:b], in_=src[:, a:b])
 
-        def regroup_s(u, c, s, a, b):
-            src, dst = views(u, c, s)
-            if b - a == 1:
-                nc.scalar.copy(out=dst[:, a], in_=src[:, a])
-            elif b > a:
-                nc.scalar.copy(out=dst[:, a:b], in_=src[:, a:b])
-
-        def regroup(u, c):
+        def regroup_unit(u):
             n = UNITS[u][1]
-            if n == 2:
-                regroup_s(u, c, 0, 0, 4)
-                if c == 1:
-                    regroup_s(u, c, 1, 0, 1)
-                    regroup_v(u, c, 1, 1, 2)
-                    regroup_v(u, c, 1, 2, 4)
-                else:
-                    regroup_v(u, c, 1, 0, 4)
+            regroup(u, 0, 0, n, nc.scalar.copy)
+            if n == 4 and u % 2 == 1:
+                regroup(u, 1, 0, 1, nc.scalar.copy)
+                regroup(u, 1, 1, 2, nc.vector.tensor_copy)
+                regroup(u, 1, 2, 4, nc.vector.tensor_copy)
             else:
-                regroup_s(u, c, 0, 0, 2)
-                regroup_v(u, c, 0, 2, 4)
+                regroup(u, 1, 0, n, nc.vector.tensor_copy)
 
-        def quant(u, c):
+        def quant_mm(u):
             w = P * UNITS[u][1]
             cod = codp.tile([P, 1024], U32, name="cod", tag="cod", align_bytes=64)
             scl = codp.tile([P, 1024], U8, name="scl", tag="scl", align_bytes=64)
             nc.vector.quantize_mx(
-                out=cod[:, 0 : 4 * w].bitcast(FP8X4), scales=scl[:, 0 : 4 * w], in_=grp[(u, c)][:, 0 : 16 * w]
+                out=cod[:, 0 : 2 * w].bitcast(FP8X4), scales=scl[:, 0 : 2 * w], in_=grp[u][:, 0 : 8 * w]
             )
-            codes[(u, c)] = (cod, scl)
-
-        def mm(u, b, tr):
-            w = P * UNITS[u][1]
-            per_bank = 1 if u == nu - 1 else 512 // w
-            k, lo = b // per_bank, (b % per_bank) * w
-            if (u, k) not in acc:
-                acc[(u, k)] = psa.tile([P, 512], F32, name="acc", tag="acc")
-            cod, scl = codes[(u, tr // 4)]
-            col = 1024 * b + P * tr
-            t = tr % 4
-            nc.tensor.matmul_mx(
-                out=acc[(u, k)][:, lo : lo + w],
-                lhsT=a_codes[:, col : col + P].bitcast(FP8X4),
-                lhsT_scale=sd[:, P * tr : P * tr + P],
-                rhs=cod[:, w * t : w * t + w].bitcast(FP8X4),
-                rhs_scale=scl[:, w * t : w * t + w],
-                start=(tr == 0),
-                stop=(tr == 7),
-            )
-
-        def mm_unit(u):
-            for b in range(4):
-                for tr in range(8):
-                    mm(u, b, tr)
+            acc[u] = psa.tile([P, 512], F32, name="acc", tag="acc")
+            for x in range(2):
+                nc.tensor.matmul_mx(
+                    out=acc[u][:, 0:w],
+                    lhsT=a_codes[:, P * x : P * x + P].bitcast(FP8X4),
+                    lhsT_scale=a_scl[:, P * x : P * x + P],
+                    rhs=cod[:, w * x : w * x + w].bitcast(FP8X4),
+                    rhs_scale=scl[:, w * x : w * x + w],
+                    start=(x == 0),
+                    stop=(x == 1),
+                )
 
         def add(u):
             n = UNITS[u][1]
-            w = P * n
-            per_bank = 1 if u == nu - 1 else 512 // w
-            ys[u] = yp.tile([P, n, 4, P], F32, name="y", tag="y")
-            for k in range(4 // per_bank):
-                nc.vector.tensor_tensor(
-                    out=ys[u][:, :, per_bank * k : per_bank * (k + 1), :].rearrange("p s b d -> p b s d"),
-                    in0=acc[(u, k)][:, 0 : per_bank * w].rearrange("p (b s d) -> p b s d", b=per_bank, s=n),
-                    in1=bias[:].unsqueeze(1).unsqueeze(1).to_broadcast([P, per_bank, n, P]),
-                    op=ALU.add,
-                )
+            ys[u] = yp.tile([P, n, P], F32, name="y", tag="y")
+            nc.vector.tensor_tensor(
+                out=ys[u][:],
+                in0=acc[u][:, 0 : P * n].rearrange("p (b d) -> p b d", b=n),
+                in1=bias[:].unsqueeze(1).to_broadcast([P, n, P]),
+                op=ALU.add,
+            )
 
         def relu(u):
-            yf = ys[u][:].rearrange("p s b d -> p (s b d)")
+            yf = ys[u][:].rearrange("p b d -> p (b d)")
             nc.scalar.activation(out=yf, in_=yf, func=ACT.Relu)
 
         def store(u):
-            g0, n = UNITS[u]
-            nc.sync.dma_start(
-                out=ov[:, 4 * g0 : 4 * (g0 + n), :], in_=ys[u][:].rearrange("p s b d -> p (s b) d")
-            )
+            b0, n = UNITS[u]
+            nc.scalar.dma_start(out=ov[:, b0 : b0 + n, :], in_=ys[u][:])
 
-        warm = const.tile([P, 16], F32, name="warm")
-        nc.gpsimd.memset(warm[:], 0.0)
-        make_identity(nc, ident[:])
-        nc.gpsimd.memset(a_codes[:, 0:2048].bitcast(I32), 0)
-        nc.vector.memset(a_codes[:, 2048:4096].bitcast(I32), 0)
         nc.sync.dma_start(out=gcw[:], in_=GCW)
         nc.sync.dma_start(out=msk[:], in_=AA_mask)
-        load(0, 0, 0, 4)
-        load(0, 1, 0, 4)
-        load(0, 0, 4, 8)
-        load(0, 1, 4, 8)
-        load_group(1)
-        nc.scalar.activation(out=warm[:], in_=warm[:], func=ACT.Relu)
+        for b in range(2):
+            load(b)
         nc.sync.dma_start(out=gcb[:], in_=GCB)
-        load_group(2)
+        for b in range(2, 64):
+            load(b)
+        nc.gpsimd.memset(warm[:], 0.0)
+        make_identity(nc, ident[:])
+        nc.scalar.activation(out=warm[:], in_=warm[:], func=ACT.Relu)
         nc.vector.tensor_copy(
             out=perm[:].rearrange("p (s t) -> p s t", s=8), in_=ident[:].rearrange("p (t s) -> p s t", s=8)
         )
-        nc.vector.scalar_tensor_tensor(out=pm[:], in0=gcw[:], scalar=0.0, in1=msk[:], op0=ALU.max, op1=ALU.mult)
-
-        pa = grpp.tile([P, 4096], BF16, name="pa", tag="grp", align_bytes=64)
-        gd = grpp.tile([P, 4096], BF16, name="gd", tag="grp", align_bytes=64)
-        paw = pa[:].bitcast(F32)
-        gdw = gd[:].bitcast(F32)
-        pav = paw.rearrange("p (t w u b c) -> p w u t b c", t=8, w=2, u=2, b=4, c=16)
-        pmv = pm[:].bitcast(F32).rearrange("p (u t c w) -> p w u t c", u=2, t=8, c=16, w=2)
-        for w in range(2):
-            for u in range(2):
-                dst = pav[:, w, u]
-                src = pmv[:, w, u].unsqueeze(2).to_broadcast([P, 8, 4, 16])
-                if u == 0:
-                    nc.vector.tensor_copy(out=dst, in_=src)
-                else:
-                    nc.scalar.copy(out=dst, in_=src)
         nc.vector.tensor_copy(out=permb[:], in_=perm[:])
-        banks = []
-        for k in range(4):
-            bank = psa.tile([P, 2, 2, P], F32, name="at", tag="acc")
-            for t in range(2):
-                for w in range(2):
-                    lo = (2 * k + t) * 256 + w * P
-                    nc.tensor.transpose(out=bank[:, t, w, :], in_=paw[:, lo : lo + P], identity=perm[:])
-            banks.append(bank)
+        nc.vector.scalar_tensor_tensor(out=am[:], in0=gcw[:], scalar=0.0, in1=msk[:], op0=ALU.max, op1=ALU.mult)
+        nc.vector.tensor_copy(
+            out=pm[:].bitcast(F32).rearrange("p (x w t c) -> p x w t c", x=2, w=2, t=16, c=8),
+            in_=am[:].bitcast(F32).rearrange("p (t x c w) -> p x w t c", x=2, w=2, t=16, c=8),
+        )
+        bank = psa.tile([P, 2, 2, P], F32, name="at", tag="acc")
+        pmw = pm[:].bitcast(F32)
+        for x in range(2):
+            for w in range(2):
+                lo = (2 * x + w) * P
+                nc.tensor.transpose(out=bank[:, x, w, :], in_=pmw[:, lo : lo + P], identity=perm[:])
         bps = psa.tile([P, 512], F32, name="bps", tag="acc")
         nc.tensor.matmul(out=bps[:, 0:P], lhsT=permb[:], rhs=gcb[:], start=True, stop=True)
-        regroup(0, 0)
-        for k in range(4):
-            dst = gdw[:, 512 * k : 512 * k + 512].rearrange("p (t m w) -> p t m w", t=2, m=P, w=2)
-            src = banks[k][:].rearrange("p t w m -> p t m w")
-            if k % 2 == 0:
-                nc.vector.tensor_copy(out=dst, in_=src)
-            else:
-                nc.scalar.copy(out=dst, in_=src)
-        load_group(3)
-        nc.vector.quantize_mx(out=cd[:].bitcast(FP8X4), scales=sd[:], in_=gd[:])
-        for u in range(2):
-            for b in range(4):
-                lo = 64 * u + 16 * b
-                nc.sync.dma_start(
-                    out=a_codes[lo : lo + 16, 1024 * b : 1024 * b + 1024].bitcast(I32),
-                    in_=cd[lo : lo + 16, :].bitcast(I32),
-                )
+        nc.vector.tensor_copy(
+            out=gd[:].bitcast(F32).rearrange("p (x m w) -> p x m w", x=2, m=P, w=2),
+            in_=bank[:].rearrange("p x w m -> p x m w"),
+        )
         nc.vector.tensor_copy(out=bias[:], in_=bps[:, 0:P])
-        regroup(0, 1)
-        quant(0, 0)
+        nc.vector.quantize_mx(out=a_codes[:].bitcast(FP8X4), scales=a_scl[:], in_=gd[:])
+        regroup_unit(0)
 
         for u in range(1, nu):
-            g0, n = UNITS[u]
-            for g in range(g0 + 3, g0 + 3 + n):
-                if g < 16:
-                    load_group(g)
-            regroup(u, 0)
-            quant(u - 1, 1)
-            mm_unit(u - 1)
+            regroup_unit(u)
+            if u >= 4:
+                store(u - 4)
             if u >= 3:
                 relu(u - 3)
-                store(u - 3)
-            regroup(u, 1)
+            quant_mm(u - 1)
             if u >= 2:
                 add(u - 2)
-            quant(u, 0)
 
-        for tr in range(4):
-            for b in range(4):
-                mm(nu - 1, b, tr)
+        store(nu - 4)
         relu(nu - 3)
+        quant_mm(nu - 1)
         store(nu - 3)
-        quant(nu - 1, 1)
         add(nu - 2)
         relu(nu - 2)
         store(nu - 2)
-        for tr in range(4, 8):
-            for b in range(4):
-                mm(nu - 1, b, tr)
         add(nu - 1)
         relu(nu - 1)
         store(nu - 1)

@@ -7,28 +7,31 @@ BF16 = mybir.dt.bfloat16
 F32 = mybir.dt.float32
 U32 = mybir.dt.uint32
 U8 = mybir.dt.uint8
+I32 = mybir.dt.int32
 FP8X4 = mybir.dt.float8_e4m3fn_x4
 ALU = mybir.AluOpType
 ACT = mybir.ActivationFunctionType
 
 P = 128
 FLOPS = 2 * 64 * 128 * 1024 * 128
-UNITS = [(a, 4) for a in range(0, 60, 4)] + [(60, 2), (62, 2)]
+ORDER = [0, 15] + list(range(1, 15))
+NG = 16
+RING = 5
+T0, T15, TZ = RING, RING + 1, RING + 2
+AHEAD = 5
 
 
 def tile_gcnfast_t_kernel(tc, h, e, AA_mask, GCW, GCB, out):
     nc = tc.nc
-    nu = len(UNITS)
     with ExitStack() as ctx:
         ctx.enter_context(tc.manual_schedule())
         const = ctx.enter_context(tc.tile_pool(name="const", bufs=1))
-        rawp = ctx.enter_context(tc.tile_pool(name="rawp", bufs=1))
+        rawp = ctx.enter_context(tc.tile_pool(name="rawp", bufs=9))
         grpp = ctx.enter_context(tc.tile_pool(name="grpp", bufs=4))
-        codp = ctx.enter_context(tc.tile_pool(name="codp", bufs=4))
-        yp = ctx.enter_context(tc.tile_pool(name="yp", bufs=6))
+        yp = ctx.enter_context(tc.tile_pool(name="yp", bufs=5))
         psa = ctx.enter_context(tc.psum_pool(name="psa", bufs=8))
 
-        hv = h.rearrange("b (x c) t d -> b x t c d", x=2)
+        hv = h.rearrange("b (c j) (u t) d -> u (b c) j (t d)", j=4, u=2)
         ov = out.rearrange("b s t d -> (s t) b d")
 
         ident = const.tile([P, P], F32, name="ident")
@@ -36,139 +39,209 @@ def tile_gcnfast_t_kernel(tc, h, e, AA_mask, GCW, GCB, out):
         permb = const.tile([P, P], BF16, name="permb")
         gcw = const.tile([P, 1024], BF16, name="gcw")
         msk = const.tile([P, 1024], BF16, name="msk")
-        am = const.tile([P, 1024], BF16, name="am")
         pm = const.tile([P, 1024], BF16, name="pm")
         gcb = const.tile([P, P], BF16, name="gcb")
         bias = const.tile([P, P], F32, name="bias")
         warm = const.tile([P, 16], F32, name="warm")
-        gd = const.tile([P, 1024], BF16, name="gd", align_bytes=64)
-        a_codes = const.tile([P, 256], U32, name="a_codes", align_bytes=64)
-        a_scl = const.tile([P, 256], U8, name="a_scl", align_bytes=64)
-        raw = rawp.tile([P, 64, 2, 4, P], BF16, name="raw")
+        cd = const.tile([P, 1024], U32, name="cd", align_bytes=64)
+        a_scl = const.tile([P, 2, 1024], U8, name="a_scl", align_bytes=64)
+        a_codes = const.tile([P, 2, 4096], U32, name="a_codes", align_bytes=64)
+        cods = const.tile([P, RING + 3, 1280], U32, name="cods", align_bytes=64)
 
+        raw = {}
         grp = {}
         acc = {}
-        codes = {}
         ys = {}
 
-        def load(b):
-            for x in range(2):
-                nc.sync.dma_start(out=raw[:, b, x, :, :], in_=hv[b, x])
+        def slot(g):
+            return T0 if g == 0 else T15 if g == 15 else g % RING
 
-        def views(u, x):
-            b0, n = UNITS[u]
-            if u not in grp:
-                grp[u] = grpp.tile([P, 4096], BF16, name="grp", tag="grp", align_bytes=64)
-            src = raw[:, b0 : b0 + n, x, :, :].rearrange("p b j (c i) -> p b c j i", i=4)
-            dst = grp[u][:, 512 * n * x : 512 * n * (x + 1)].rearrange("p (b c i j) -> p b c j i", b=n, c=32, i=4, j=4)
-            return src, dst
+        def load(g):
+            raw[g] = rawp.tile([P, 4, 8, P], BF16, name="raw", tag="raw")
+            u = g % 2
+            flat = raw[g][:].rearrange("p j t d -> p j (t d)")
+            if g == 0:
+                for a in range(2):
+                    nc.sync.dma_start(
+                        out=flat[:, :, 512 * a : 512 * a + 512], in_=hv[0, 0:P, :, 512 * a : 512 * a + 512]
+                    )
+            elif g == 15:
+                nc.sync.dma_start(out=flat[0:64], in_=hv[u, 960:1024])
+                nc.sync.dma_start(out=flat[64:128], in_=hv[u, 0:64])
+            else:
+                nc.sync.dma_start(out=flat, in_=hv[u, 64 * g : 64 * g + P])
 
-        def regroup(u, x, a, b, op):
-            src, dst = views(u, x)
+        def regroup(g, a, b, op):
+            if g not in grp:
+                grp[g] = grpp.tile([P, 4096], BF16, name="grp", tag="grp", align_bytes=64)
+            src = raw[g][:].rearrange("p j t (c i) -> p t c j i", i=4)
+            dst = grp[g][:].rearrange("p (t c i j) -> p t c j i", t=8, c=32, i=4, j=4)
             if b - a == 1:
                 op(out=dst[:, a], in_=src[:, a])
             elif b > a:
                 op(out=dst[:, a:b], in_=src[:, a:b])
 
-        def regroup_unit(u):
-            n = UNITS[u][1]
-            regroup(u, 0, 0, n, nc.scalar.copy)
-            if n == 4 and u % 2 == 1:
-                regroup(u, 1, 0, 1, nc.scalar.copy)
-                regroup(u, 1, 1, 2, nc.vector.tensor_copy)
-                regroup(u, 1, 2, 4, nc.vector.tensor_copy)
-            else:
-                regroup(u, 1, 0, n, nc.vector.tensor_copy)
+        def v_pieces(g):
+            return 2 + g % 2
 
-        def quant_mm(u):
-            w = P * UNITS[u][1]
-            cod = codp.tile([P, 1024], U32, name="cod", tag="cod", align_bytes=64)
-            scl = codp.tile([P, 1024], U8, name="scl", tag="scl", align_bytes=64)
+        def regroup_s(g):
+            regroup(g, v_pieces(g), 8, nc.scalar.copy)
+
+        def regroup_v(g):
+            regroup(g, 0, 2, nc.vector.tensor_copy)
+            regroup(g, 2, v_pieces(g), nc.vector.tensor_copy)
+
+        def quant(g):
+            k = slot(g)
             nc.vector.quantize_mx(
-                out=cod[:, 0 : 2 * w].bitcast(FP8X4), scales=scl[:, 0 : 2 * w], in_=grp[u][:, 0 : 8 * w]
+                out=cods[:, k, 0:1024].bitcast(FP8X4), scales=cods[:, k, 1024:1280].bitcast(U8), in_=grp[g][:]
             )
-            acc[u] = psa.tile([P, 512], F32, name="acc", tag="acc")
-            for x in range(2):
-                nc.tensor.matmul_mx(
-                    out=acc[u][:, 0:w],
-                    lhsT=a_codes[:, P * x : P * x + P].bitcast(FP8X4),
-                    lhsT_scale=a_scl[:, P * x : P * x + P],
-                    rhs=cod[:, w * x : w * x + w].bitcast(FP8X4),
-                    rhs_scale=scl[:, w * x : w * x + w],
-                    start=(x == 0),
-                    stop=(x == 1),
-                )
 
-        def add(u):
-            n = UNITS[u][1]
-            ys[u] = yp.tile([P, n, P], F32, name="y", tag="y")
+        def move(half, k_from, k_to):
+            p = slice(64 * half, 64 * half + 64)
+            nc.vector.tensor_copy(out=cods[p, k_to, :].bitcast(I32), in_=cods[p, k_from, :].bitcast(I32))
+
+        def mm(s, k, b, tr, bank, lo):
+            par = s % 2
+            nc.tensor.matmul_mx(
+                out=bank[:, lo : lo + P],
+                lhsT=a_codes[:, par, 1024 * b + P * tr : 1024 * b + P * tr + P].bitcast(FP8X4),
+                lhsT_scale=a_scl[:, par, P * tr : P * tr + P],
+                rhs=cods[:, k, P * tr : P * tr + P].bitcast(FP8X4),
+                rhs_scale=cods[:, k, 1024:1280].bitcast(U8)[:, P * tr : P * tr + P],
+                start=(tr == 0),
+                stop=(tr == 7),
+            )
+
+        def mm_group(s, k):
+            acc[s] = psa.tile([P, 512], F32, name="acc", tag="acc")
+            for b in range(4):
+                for tr in range(8):
+                    mm(s, k, b, tr, acc[s], P * b)
+
+        def add(s):
+            ys[s] = yp.tile([P, 4, P], F32, name="y", tag="y")
             nc.vector.tensor_tensor(
-                out=ys[u][:],
-                in0=acc[u][:, 0 : P * n].rearrange("p (b d) -> p b d", b=n),
-                in1=bias[:].unsqueeze(1).to_broadcast([P, n, P]),
+                out=ys[s][:],
+                in0=acc[s][:].rearrange("p (b d) -> p b d", b=4),
+                in1=bias[:].unsqueeze(1).to_broadcast([P, 4, P]),
                 op=ALU.add,
             )
 
-        def relu(u):
-            yf = ys[u][:].rearrange("p b d -> p (b d)")
+        def relu(s):
+            yf = ys[s][:].rearrange("p b d -> p (b d)")
             nc.scalar.activation(out=yf, in_=yf, func=ACT.Relu)
 
-        def store(u):
-            b0, n = UNITS[u]
-            nc.scalar.dma_start(out=ov[:, b0 : b0 + n, :], in_=ys[u][:])
+        def store(s):
+            nc.sync.dma_start(out=ov[:, 4 * s : 4 * s + 4, :], in_=ys[s][:])
 
-        nc.sync.dma_start(out=gcw[:], in_=GCW)
-        nc.sync.dma_start(out=msk[:], in_=AA_mask)
-        for b in range(2):
-            load(b)
-        nc.sync.dma_start(out=gcb[:], in_=GCB)
-        for b in range(2, 64):
-            load(b)
         nc.gpsimd.memset(warm[:], 0.0)
         make_identity(nc, ident[:])
+        nc.gpsimd.memset(a_codes[:, 0, 2560:4096].bitcast(I32), 0)
+        nc.gpsimd.memset(a_scl[:, 1, :].bitcast(I32), 0)
+        nc.gpsimd.memset(a_codes[:, 1, 2048:4096].bitcast(I32), 0)
+        nc.vector.memset(a_codes[:, 0, 0:2560].bitcast(I32), 0)
+        nc.sync.dma_start(out=gcw[:], in_=GCW)
+        nc.sync.dma_start(out=msk[:], in_=AA_mask)
+        load(0)
+        nc.sync.dma_start(out=gcb[:], in_=GCB)
+        for g in ORDER[1:AHEAD]:
+            load(g)
         nc.scalar.activation(out=warm[:], in_=warm[:], func=ACT.Relu)
+        nc.vector.scalar_tensor_tensor(out=pm[:], in0=gcw[:], scalar=0.0, in1=msk[:], op0=ALU.max, op1=ALU.mult)
+
+        pa = grpp.tile([P, 4096], BF16, name="pa", tag="grp", align_bytes=64)
+        gd = grpp.tile([P, 4096], BF16, name="gd", tag="grp", align_bytes=64)
+        paw = pa[:].bitcast(F32)
+        gdw = gd[:].bitcast(F32)
+        pav = paw.rearrange("p (t w u b c) -> p w u t b c", t=8, w=2, u=2, b=4, c=16)
+        pmv = pm[:].bitcast(F32).rearrange("p (u t c w) -> p w u t c", u=2, t=8, c=16, w=2)
+        for w in range(2):
+            for u in range(2):
+                dst = pav[:, w, u]
+                src = pmv[:, w, u].unsqueeze(2).to_broadcast([P, 8, 4, 16])
+                if u == 0:
+                    nc.vector.tensor_copy(out=dst, in_=src)
+                else:
+                    nc.scalar.copy(out=dst, in_=src)
         nc.vector.tensor_copy(
             out=perm[:].rearrange("p (s t) -> p s t", s=8), in_=ident[:].rearrange("p (t s) -> p s t", s=8)
         )
         nc.vector.tensor_copy(out=permb[:], in_=perm[:])
-        nc.vector.scalar_tensor_tensor(out=am[:], in0=gcw[:], scalar=0.0, in1=msk[:], op0=ALU.max, op1=ALU.mult)
-        nc.vector.tensor_copy(
-            out=pm[:].bitcast(F32).rearrange("p (x w t c) -> p x w t c", x=2, w=2, t=16, c=8),
-            in_=am[:].bitcast(F32).rearrange("p (t x c w) -> p x w t c", x=2, w=2, t=16, c=8),
-        )
-        bank = psa.tile([P, 2, 2, P], F32, name="at", tag="acc")
-        pmw = pm[:].bitcast(F32)
-        for x in range(2):
-            for w in range(2):
-                lo = (2 * x + w) * P
-                nc.tensor.transpose(out=bank[:, x, w, :], in_=pmw[:, lo : lo + P], identity=perm[:])
+        banks = []
+        for k in range(4):
+            bank = psa.tile([P, 2, 2, P], F32, name="at", tag="acc")
+            for t in range(2):
+                for w in range(2):
+                    lo = (2 * k + t) * 256 + w * P
+                    nc.tensor.transpose(out=bank[:, t, w, :], in_=paw[:, lo : lo + P], identity=perm[:])
+            banks.append(bank)
         bps = psa.tile([P, 512], F32, name="bps", tag="acc")
         nc.tensor.matmul(out=bps[:, 0:P], lhsT=permb[:], rhs=gcb[:], start=True, stop=True)
-        nc.vector.tensor_copy(
-            out=gd[:].bitcast(F32).rearrange("p (x m w) -> p x m w", x=2, m=P, w=2),
-            in_=bank[:].rearrange("p x w m -> p x m w"),
-        )
+        nc.vector.memset(cods[:, :, 1024:1280].bitcast(I32), 0)
+        nc.vector.memset(a_codes[:, 1, 0:2048].bitcast(I32), 0)
+        regroup_s(0)
+        for k in range(4):
+            dst = gdw[:, 512 * k : 512 * k + 512].rearrange("p (t m w) -> p t m w", t=2, m=P, w=2)
+            src = banks[k][:].rearrange("p t w m -> p t m w")
+            nc.vector.tensor_copy(out=dst, in_=src)
         nc.vector.tensor_copy(out=bias[:], in_=bps[:, 0:P])
-        nc.vector.quantize_mx(out=a_codes[:].bitcast(FP8X4), scales=a_scl[:], in_=gd[:])
-        regroup_unit(0)
+        nc.vector.quantize_mx(out=cd[:].bitcast(FP8X4), scales=a_scl[:, 0, :], in_=gd[:])
+        for par in range(2):
+            for u in range(2):
+                for b in range(4):
+                    lo = 64 * u + 16 * b
+                    fr = 64 * (u ^ par) + 16 * b
+                    nc.sync.dma_start(
+                        out=a_codes[lo : lo + 16, par, 1024 * b : 1024 * b + 1024].bitcast(I32),
+                        in_=cd[fr : fr + 16, :].bitcast(I32),
+                    )
+        for q in range(4):
+            lo, fr = 32 * q, 32 * (q ^ 2)
+            nc.sync.dma_start(
+                out=a_scl[lo : lo + 4, 1, :].bitcast(I32), in_=a_scl[fr : fr + 4, 0, :].bitcast(I32)
+            )
+        regroup_v(0)
 
-        for u in range(1, nu):
-            regroup_unit(u)
-            if u >= 4:
-                store(u - 4)
-            if u >= 3:
-                relu(u - 3)
-            quant_mm(u - 1)
-            if u >= 2:
-                add(u - 2)
+        done = []
 
-        store(nu - 4)
-        relu(nu - 3)
-        quant_mm(nu - 1)
-        store(nu - 3)
-        add(nu - 2)
-        relu(nu - 2)
-        store(nu - 2)
-        add(nu - 1)
-        relu(nu - 1)
-        store(nu - 1)
+        def complete(g):
+            if g == 15:
+                move(1, T0, TZ)
+                move(1, T15, T0)
+                done.append((0, T0))
+            elif g > 0:
+                k = TZ if g == 1 else (g - 1) % RING
+                move(0, slot(g), k)
+                done.append((g, k))
+                if g == 14:
+                    move(1, slot(g), T15)
+                    done.append((15, T15))
+
+        n_mm = 0
+        for j in range(1, NG):
+            if j + AHEAD - 1 < NG:
+                load(ORDER[j + AHEAD - 1])
+            regroup_s(ORDER[j])
+            if j >= 5:
+                relu(j - 5)
+                store(j - 5)
+            regroup_v(ORDER[j])
+            quant(ORDER[j - 1])
+            if j >= 4:
+                add(j - 4)
+            complete(ORDER[j - 1])
+            for s, k in done[n_mm:]:
+                mm_group(s, k)
+            n_mm = len(done)
+
+        quant(ORDER[NG - 1])
+        add(NG - 4)
+        complete(ORDER[NG - 1])
+        for s, k in done[n_mm:]:
+            mm_group(s, k)
+        for s in range(NG - 5, NG):
+            if s > NG - 4:
+                add(s)
+            relu(s)
+            store(s)

@@ -14,7 +14,7 @@ ACT = mybir.ActivationFunctionType
 
 P = 128
 FLOPS = 2 * 64 * 128 * 1024 * 128
-ORDER = [0, 15] + list(range(1, 15))
+ORDER = [0, 1, 2, 3, 15] + list(range(4, 15))
 NG = 16
 RING = 5
 T0, T15, TZ = RING, RING + 1, RING + 2
@@ -97,6 +97,22 @@ def tile_gcnfast_t_kernel(tc, h, e, AA_mask, GCW, GCB, out):
                 out=cods[:, k, 0:1024].bitcast(FP8X4), scales=cods[:, k, 1024:1280].bitcast(U8), in_=grp[g][:]
             )
 
+        def quant_part(g, a):
+            k = slot(g)
+            scl = cods[:, k, 1024:1280].bitcast(U8)
+            nc.vector.quantize_mx(
+                out=cods[:, k, 512 * a : 512 * a + 512].bitcast(FP8X4),
+                scales=scl[:, 512 * a : 512 * a + 512],
+                in_=grp[g][:, 2048 * a : 2048 * a + 2048],
+            )
+
+        def move_part(half, k_from, k_to, a):
+            p = slice(64 * half, 64 * half + 64)
+            for lo, w in ((512 * a, 512), (1024 + 128 * a, 128)):
+                nc.vector.tensor_copy(
+                    out=cods[p, k_to, lo : lo + w].bitcast(I32), in_=cods[p, k_from, lo : lo + w].bitcast(I32)
+                )
+
         def move(half, k_from, k_to):
             p = slice(64 * half, 64 * half + 64)
             nc.vector.tensor_copy(out=cods[p, k_to, :].bitcast(I32), in_=cods[p, k_from, :].bitcast(I32))
@@ -137,16 +153,20 @@ def tile_gcnfast_t_kernel(tc, h, e, AA_mask, GCW, GCB, out):
 
         nc.gpsimd.memset(warm[:], 0.0)
         make_identity(nc, ident[:])
-        nc.gpsimd.memset(a_codes[:, 0, 2560:4096].bitcast(I32), 0)
+        for a in range(4):
+            nc.gpsimd.memset(a_codes[:, 0, 2048 + 512 * a : 2560 + 512 * a].bitcast(I32), 0)
         nc.gpsimd.memset(a_scl[:, 1, :].bitcast(I32), 0)
-        nc.gpsimd.memset(a_codes[:, 1, 2048:4096].bitcast(I32), 0)
-        nc.vector.memset(a_codes[:, 0, 0:2560].bitcast(I32), 0)
+        for k in range(RING + 3):
+            nc.gpsimd.memset(cods[:, k, 1024:1280].bitcast(I32), 0)
+        for a in range(4):
+            nc.gpsimd.memset(a_codes[:, 1, 512 * a : 512 * a + 512].bitcast(I32), 0)
+        nc.vector.memset(a_codes[:, 0, 0:2048].bitcast(I32), 0)
         nc.sync.dma_start(out=gcw[:], in_=GCW)
         nc.sync.dma_start(out=msk[:], in_=AA_mask)
         load(0)
         nc.sync.dma_start(out=gcb[:], in_=GCB)
-        for g in ORDER[1:AHEAD]:
-            load(g)
+        load(1)
+        load(2)
         nc.scalar.activation(out=warm[:], in_=warm[:], func=ACT.Relu)
         nc.vector.scalar_tensor_tensor(out=pm[:], in0=gcw[:], scalar=0.0, in1=msk[:], op0=ALU.max, op1=ALU.mult)
 
@@ -178,70 +198,114 @@ def tile_gcnfast_t_kernel(tc, h, e, AA_mask, GCW, GCB, out):
             banks.append(bank)
         bps = psa.tile([P, 512], F32, name="bps", tag="acc")
         nc.tensor.matmul(out=bps[:, 0:P], lhsT=permb[:], rhs=gcb[:], start=True, stop=True)
-        nc.vector.memset(cods[:, :, 1024:1280].bitcast(I32), 0)
-        nc.vector.memset(a_codes[:, 1, 0:2048].bitcast(I32), 0)
-        regroup_s(0)
         for k in range(4):
             dst = gdw[:, 512 * k : 512 * k + 512].rearrange("p (t m w) -> p t m w", t=2, m=P, w=2)
             src = banks[k][:].rearrange("p t w m -> p t m w")
-            nc.vector.tensor_copy(out=dst, in_=src)
-        nc.vector.tensor_copy(out=bias[:], in_=bps[:, 0:P])
+            if k % 2 == 0:
+                nc.vector.tensor_copy(out=dst, in_=src)
+            else:
+                nc.scalar.copy(out=dst, in_=src)
+        regroup_s(0)
         nc.vector.quantize_mx(out=cd[:].bitcast(FP8X4), scales=a_scl[:, 0, :], in_=gd[:])
-        for par in range(2):
-            for u in range(2):
-                for b in range(4):
+        nc.vector.tensor_copy(out=bias[:], in_=bps[:, 0:P])
+
+        def place_weights(par):
+            for b in range(4):
+                for u in range(2):
                     lo = 64 * u + 16 * b
                     fr = 64 * (u ^ par) + 16 * b
                     nc.sync.dma_start(
                         out=a_codes[lo : lo + 16, par, 1024 * b : 1024 * b + 1024].bitcast(I32),
                         in_=cd[fr : fr + 16, :].bitcast(I32),
                     )
+
+        place_weights(0)
+        load(3)
+        nc.vector.memset(a_codes[:, 1, 2048:4096].bitcast(I32), 0)
+        place_weights(1)
         for q in range(4):
             lo, fr = 32 * q, 32 * (q ^ 2)
             nc.sync.dma_start(
                 out=a_scl[lo : lo + 4, 1, :].bitcast(I32), in_=a_scl[fr : fr + 4, 0, :].bitcast(I32)
             )
+        load(15)
         regroup_v(0)
 
         done = []
 
         def complete(g):
-            if g == 15:
+            if g == 1:
                 move(1, T0, TZ)
+                move(0, slot(1), TZ)
+                done.append((1, TZ))
+            elif g == 15:
                 move(1, T15, T0)
                 done.append((0, T0))
-            elif g > 0:
-                k = TZ if g == 1 else (g - 1) % RING
-                move(0, slot(g), k)
-                done.append((g, k))
+            elif g > 1:
+                move(0, slot(g), slot(g - 1))
+                done.append((g, slot(g - 1)))
                 if g == 14:
                     move(1, slot(g), T15)
                     done.append((15, T15))
 
         n_mm = 0
-        for j in range(1, NG):
+        n_add = 0
+        n_out = 0
+        for j in range(1, NG - 1):
             if j + AHEAD - 1 < NG:
                 load(ORDER[j + AHEAD - 1])
             regroup_s(ORDER[j])
-            if j >= 5:
-                relu(j - 5)
-                store(j - 5)
+            if n_out < n_add:
+                relu(done[n_out][0])
+                store(done[n_out][0])
+                n_out += 1
             regroup_v(ORDER[j])
             quant(ORDER[j - 1])
-            if j >= 4:
-                add(j - 4)
+            if n_add < n_mm - 1:
+                add(done[n_add][0])
+                n_add += 1
             complete(ORDER[j - 1])
             for s, k in done[n_mm:]:
                 mm_group(s, k)
             n_mm = len(done)
 
-        quant(ORDER[NG - 1])
-        add(NG - 4)
-        complete(ORDER[NG - 1])
-        for s, k in done[n_mm:]:
-            mm_group(s, k)
-        for s in range(NG - 5, NG):
-            if s > NG - 4:
-                add(s)
+        last = ORDER[NG - 1]
+        k = slot(last)
+        regroup(last, 2, 4, nc.scalar.copy)
+        relu(done[n_out][0])
+        store(done[n_out][0])
+        n_out += 1
+        regroup(last, 0, 2, nc.vector.tensor_copy)
+        quant(ORDER[NG - 2])
+        add(done[n_add][0])
+        n_add += 1
+        complete(ORDER[NG - 2])
+        for s, kk in done[n_mm:]:
+            mm_group(s, kk)
+        n_mm = len(done)
+        regroup(last, 6, 8, nc.scalar.copy)
+        regroup(last, 4, 6, nc.vector.tensor_copy)
+        ends = [(14, slot(13), 0), (15, T15, 1)]
+        banks = {}
+        for a in range(2):
+            quant_part(last, a)
+            while n_add < n_mm - 1 + a:
+                add(done[n_add][0])
+                n_add += 1
+            for s, kt, half in ends:
+                move_part(half, k, kt, a)
+                for tr in range(4 * a, 4 * a + 4):
+                    for b in range(4):
+                        if tr == 0:
+                            banks[(s, b)] = psa.tile([P, 512], F32, name="acc", tag="acc")
+                        mm(s, kt, b, tr, banks[(s, b)], 0)
+        while n_out < n_add:
+            relu(done[n_out][0])
+            store(done[n_out][0])
+            n_out += 1
+        for s, kt, half in ends:
+            ys[s] = yp.tile([P, 4, P], F32, name="y", tag="y")
+            for b in range(4):
+                nc.vector.tensor_tensor(out=ys[s][:, b, :], in0=banks[(s, b)][:, 0:P], in1=bias[:], op=ALU.add)
             relu(s)
             store(s)

@@ -82,7 +82,7 @@ def tile_gcnfast_t_kernel(tc, h, e, AA_mask, GCW, GCB, out):
                 op(out=dst[:, a:b], in_=src[:, a:b])
 
         def v_pieces(g):
-            return 2 + g % 2
+            return 3
 
         def regroup_s(g):
             regroup(g, v_pieces(g), 8, nc.scalar.copy)
@@ -153,14 +153,10 @@ def tile_gcnfast_t_kernel(tc, h, e, AA_mask, GCW, GCB, out):
 
         nc.gpsimd.memset(warm[:], 0.0)
         make_identity(nc, ident[:])
-        for a in range(4):
-            nc.gpsimd.memset(a_codes[:, 0, 2048 + 512 * a : 2560 + 512 * a].bitcast(I32), 0)
         nc.gpsimd.memset(a_scl[:, 1, :].bitcast(I32), 0)
-        for k in range(RING + 3):
-            nc.gpsimd.memset(cods[:, k, 1024:1280].bitcast(I32), 0)
         for a in range(4):
             nc.gpsimd.memset(a_codes[:, 1, 512 * a : 512 * a + 512].bitcast(I32), 0)
-        nc.vector.memset(a_codes[:, 0, 0:2048].bitcast(I32), 0)
+        nc.vector.memset(a_codes[:, 0, :].bitcast(I32), 0)
         nc.sync.dma_start(out=gcw[:], in_=GCW)
         nc.sync.dma_start(out=msk[:], in_=AA_mask)
         load(0)
@@ -184,6 +180,7 @@ def tile_gcnfast_t_kernel(tc, h, e, AA_mask, GCW, GCB, out):
                     nc.vector.tensor_copy(out=dst, in_=src)
                 else:
                     nc.scalar.copy(out=dst, in_=src)
+        regroup_s(0)
         nc.vector.tensor_copy(
             out=perm[:].rearrange("p (s t) -> p s t", s=8), in_=ident[:].rearrange("p (t s) -> p s t", s=8)
         )
@@ -201,11 +198,7 @@ def tile_gcnfast_t_kernel(tc, h, e, AA_mask, GCW, GCB, out):
         for k in range(4):
             dst = gdw[:, 512 * k : 512 * k + 512].rearrange("p (t m w) -> p t m w", t=2, m=P, w=2)
             src = banks[k][:].rearrange("p t w m -> p t m w")
-            if k % 2 == 0:
-                nc.vector.tensor_copy(out=dst, in_=src)
-            else:
-                nc.scalar.copy(out=dst, in_=src)
-        regroup_s(0)
+            nc.vector.tensor_copy(out=dst, in_=src)
         nc.vector.quantize_mx(out=cd[:].bitcast(FP8X4), scales=a_scl[:, 0, :], in_=gd[:])
         nc.vector.tensor_copy(out=bias[:], in_=bps[:, 0:P])
 
@@ -222,6 +215,7 @@ def tile_gcnfast_t_kernel(tc, h, e, AA_mask, GCW, GCB, out):
         place_weights(0)
         load(3)
         nc.vector.memset(a_codes[:, 1, 2048:4096].bitcast(I32), 0)
+        nc.vector.memset(cods[:, :, 1024:1280].bitcast(I32), 0)
         place_weights(1)
         for q in range(4):
             lo, fr = 32 * q, 32 * (q ^ 2)

@@ -14,7 +14,7 @@ ACT = mybir.ActivationFunctionType
 
 P = 128
 FLOPS = 2 * 64 * 128 * 1024 * 128
-ORDER = [0, 1, 2, 3, 15] + list(range(4, 15))
+ORDER = list(range(0, 8)) + [15] + list(range(8, 15))
 NG = 16
 RING = 5
 T0, T15, TZ = RING, RING + 1, RING + 2
@@ -82,7 +82,7 @@ def tile_gcnfast_t_kernel(tc, h, e, AA_mask, GCW, GCB, out):
                 op(out=dst[:, a:b], in_=src[:, a:b])
 
         def v_pieces(g):
-            return 3
+            return 2 + g % 2
 
         def regroup_s(g):
             regroup(g, v_pieces(g), 8, nc.scalar.copy)
@@ -161,8 +161,8 @@ def tile_gcnfast_t_kernel(tc, h, e, AA_mask, GCW, GCB, out):
         nc.sync.dma_start(out=msk[:], in_=AA_mask)
         load(0)
         nc.sync.dma_start(out=gcb[:], in_=GCB)
-        load(1)
-        load(2)
+        for g in ORDER[1:AHEAD]:
+            load(g)
         nc.scalar.activation(out=warm[:], in_=warm[:], func=ACT.Relu)
         nc.vector.scalar_tensor_tensor(out=pm[:], in0=gcw[:], scalar=0.0, in1=msk[:], op0=ALU.max, op1=ALU.mult)
 
@@ -202,27 +202,33 @@ def tile_gcnfast_t_kernel(tc, h, e, AA_mask, GCW, GCB, out):
         nc.vector.quantize_mx(out=cd[:].bitcast(FP8X4), scales=a_scl[:, 0, :], in_=gd[:])
         nc.vector.tensor_copy(out=bias[:], in_=bps[:, 0:P])
 
-        def place_weights(par):
-            for b in range(4):
-                for u in range(2):
-                    lo = 64 * u + 16 * b
-                    fr = 64 * (u ^ par) + 16 * b
-                    nc.sync.dma_start(
-                        out=a_codes[lo : lo + 16, par, 1024 * b : 1024 * b + 1024].bitcast(I32),
-                        in_=cd[fr : fr + 16, :].bitcast(I32),
-                    )
+        def place_weights(par, b):
+            for u in range(2):
+                lo = 64 * u + 16 * b
+                fr = 64 * (u ^ par) + 16 * b
+                nc.sync.dma_start(
+                    out=a_codes[lo : lo + 16, par, 1024 * b : 1024 * b + 1024].bitcast(I32),
+                    in_=cd[fr : fr + 16, :].bitcast(I32),
+                )
 
-        place_weights(0)
-        load(3)
+        def place_scales():
+            for q in range(4):
+                lo, fr = 32 * q, 32 * (q ^ 2)
+                nc.sync.dma_start(
+                    out=a_scl[lo : lo + 4, 1, :].bitcast(I32), in_=a_scl[fr : fr + 4, 0, :].bitcast(I32)
+                )
+
         nc.vector.memset(a_codes[:, 1, 2048:4096].bitcast(I32), 0)
         nc.vector.memset(cods[:, :, 1024:1280].bitcast(I32), 0)
-        place_weights(1)
-        for q in range(4):
-            lo, fr = 32 * q, 32 * (q ^ 2)
-            nc.sync.dma_start(
-                out=a_scl[lo : lo + 4, 1, :].bitcast(I32), in_=a_scl[fr : fr + 4, 0, :].bitcast(I32)
-            )
-        load(15)
+        place_scales()
+        place_weights(1, 0)
+        place_weights(1, 1)
+        load(ORDER[AHEAD])
+        place_weights(1, 2)
+        place_weights(1, 3)
+        load(ORDER[AHEAD + 1])
+        for b in range(4):
+            place_weights(0, b)
         regroup_v(0)
 
         done = []
@@ -246,8 +252,8 @@ def tile_gcnfast_t_kernel(tc, h, e, AA_mask, GCW, GCB, out):
         n_add = 0
         n_out = 0
         for j in range(1, NG - 1):
-            if j + AHEAD - 1 < NG:
-                load(ORDER[j + AHEAD - 1])
+            if j + AHEAD + 1 < NG:
+                load(ORDER[j + AHEAD + 1])
             regroup_s(ORDER[j])
             if n_out < n_add:
                 relu(done[n_out][0])

@@ -28,8 +28,9 @@ def tile_gcnfast_t_kernel(tc, h, e, AA_mask, GCW, GCB, out):
         const = ctx.enter_context(tc.tile_pool(name="const", bufs=1))
         rawp = ctx.enter_context(tc.tile_pool(name="rawp", bufs=9))
         grpp = ctx.enter_context(tc.tile_pool(name="grpp", bufs=4))
-        yp = ctx.enter_context(tc.tile_pool(name="yp", bufs=5))
-        psa = ctx.enter_context(tc.psum_pool(name="psa", bufs=8))
+        yp = ctx.enter_context(tc.tile_pool(name="yp", bufs=7))
+        psa = ctx.enter_context(tc.psum_pool(name="psa", bufs=6))
+        psr = ctx.enter_context(tc.psum_pool(name="psr", bufs=2))
 
         hv = h.rearrange("b (c j) (u t) d -> u (b c) j (t d)", j=4, u=2)
         ov = out.rearrange("b s t d -> (s t) b d")
@@ -37,6 +38,7 @@ def tile_gcnfast_t_kernel(tc, h, e, AA_mask, GCW, GCB, out):
         ident = const.tile([P, P], F32, name="ident")
         perm = const.tile([P, P], F32, name="perm")
         permb = const.tile([P, P], BF16, name="permb")
+        identb = const.tile([P, P], BF16, name="identb")
         gcw = const.tile([P, 1024], BF16, name="gcw")
         msk = const.tile([P, 1024], BF16, name="msk")
         pm = const.tile([P, 1024], BF16, name="pm")
@@ -49,6 +51,7 @@ def tile_gcnfast_t_kernel(tc, h, e, AA_mask, GCW, GCB, out):
         cods = const.tile([P, RING + 3, 1280], U32, name="cods", align_bytes=64)
 
         raw = {}
+        reg = {}
         grp = {}
         acc = {}
         ys = {}
@@ -72,6 +75,8 @@ def tile_gcnfast_t_kernel(tc, h, e, AA_mask, GCW, GCB, out):
                 nc.sync.dma_start(out=flat, in_=hv[u, 64 * g : 64 * g + P])
 
         def regroup(g, a, b, op):
+            if b == a:
+                return
             if g not in grp:
                 grp[g] = grpp.tile([P, 4096], BF16, name="grp", tag="grp", align_bytes=64)
             src = raw[g][:].rearrange("p j t (c i) -> p t c j i", i=4)
@@ -82,14 +87,33 @@ def tile_gcnfast_t_kernel(tc, h, e, AA_mask, GCW, GCB, out):
                 op(out=dst[:, a:b], in_=src[:, a:b])
 
         def v_pieces(g):
-            return 2 + g % 2
+            return 0 if g == ORDER[-1] else 2 + 2 * (g % 2)
+
+        def on_tensor(g):
+            return g in ORDER[2:14]
+
+        def spread_piece(g):
+            bank = psr.tile([P, 512], BF16, name="reg", tag="reg")
+            slots = bank[:].rearrange("p (d w e) -> p w d e", d=P, w=2, e=2)
+            for w in range(2):
+                nc.tensor.matmul(
+                    out=slots[:, w],
+                    lhsT=identb[:],
+                    rhs=raw[g][:, 2 * w : 2 * w + 2, 7, :].rearrange("p e d -> p d e"),
+                    start=True,
+                    stop=True,
+                )
+            reg[g] = bank
 
         def regroup_s(g):
-            regroup(g, v_pieces(g), 8, nc.scalar.copy)
+            if on_tensor(g):
+                regroup(g, v_pieces(g), 7, nc.scalar.copy)
+                nc.scalar.copy(out=grp[g][:, 3584:4096], in_=reg[g][:])
+            else:
+                regroup(g, v_pieces(g), 8, nc.scalar.copy)
 
         def regroup_v(g):
-            regroup(g, 0, 2, nc.vector.tensor_copy)
-            regroup(g, 2, v_pieces(g), nc.vector.tensor_copy)
+            regroup(g, 0, v_pieces(g), nc.vector.tensor_copy)
 
         def quant(g):
             k = slot(g)
@@ -117,7 +141,7 @@ def tile_gcnfast_t_kernel(tc, h, e, AA_mask, GCW, GCB, out):
             p = slice(64 * half, 64 * half + 64)
             nc.vector.tensor_copy(out=cods[p, k_to, :].bitcast(I32), in_=cods[p, k_from, :].bitcast(I32))
 
-        def mm(s, k, b, tr, bank, lo):
+        def mm(s, k, b, tr, bank, lo, first=0, last=7):
             par = s % 2
             nc.tensor.matmul_mx(
                 out=bank[:, lo : lo + P],
@@ -125,8 +149,8 @@ def tile_gcnfast_t_kernel(tc, h, e, AA_mask, GCW, GCB, out):
                 lhsT_scale=a_scl[:, par, P * tr : P * tr + P],
                 rhs=cods[:, k, P * tr : P * tr + P].bitcast(FP8X4),
                 rhs_scale=cods[:, k, 1024:1280].bitcast(U8)[:, P * tr : P * tr + P],
-                start=(tr == 0),
-                stop=(tr == 7),
+                start=(tr == first),
+                stop=(tr == last),
             )
 
         def mm_group(s, k):
@@ -185,6 +209,7 @@ def tile_gcnfast_t_kernel(tc, h, e, AA_mask, GCW, GCB, out):
             out=perm[:].rearrange("p (s t) -> p s t", s=8), in_=ident[:].rearrange("p (t s) -> p s t", s=8)
         )
         nc.vector.tensor_copy(out=permb[:], in_=perm[:])
+        nc.vector.tensor_copy(out=identb[:], in_=ident[:])
         banks = []
         for k in range(4):
             bank = psa.tile([P, 2, 2, P], F32, name="at", tag="acc")
@@ -205,7 +230,7 @@ def tile_gcnfast_t_kernel(tc, h, e, AA_mask, GCW, GCB, out):
         def place_weights(par, b):
             for u in range(2):
                 lo = 64 * u + 16 * b
-                fr = 64 * (u ^ par) + 16 * b
+                fr = 64 * (u ^ par) + 16 * (b ^ 1)
                 nc.sync.dma_start(
                     out=a_codes[lo : lo + 16, par, 1024 * b : 1024 * b + 1024].bitcast(I32),
                     in_=cd[fr : fr + 16, :].bitcast(I32),
@@ -248,6 +273,7 @@ def tile_gcnfast_t_kernel(tc, h, e, AA_mask, GCW, GCB, out):
                     move(1, slot(g), T15)
                     done.append((15, T15))
 
+        spread_piece(ORDER[2])
         n_mm = 0
         n_add = 0
         n_out = 0
@@ -255,7 +281,7 @@ def tile_gcnfast_t_kernel(tc, h, e, AA_mask, GCW, GCB, out):
             if j + AHEAD + 1 < NG:
                 load(ORDER[j + AHEAD + 1])
             regroup_s(ORDER[j])
-            if n_out < n_add:
+            if n_out < n_add - 1:
                 relu(done[n_out][0])
                 store(done[n_out][0])
                 n_out += 1
@@ -265,17 +291,16 @@ def tile_gcnfast_t_kernel(tc, h, e, AA_mask, GCW, GCB, out):
                 add(done[n_add][0])
                 n_add += 1
             complete(ORDER[j - 1])
+            if j + 2 < NG and on_tensor(ORDER[j + 2]):
+                spread_piece(ORDER[j + 2])
             for s, k in done[n_mm:]:
                 mm_group(s, k)
             n_mm = len(done)
 
         last = ORDER[NG - 1]
         k = slot(last)
-        regroup(last, 2, 4, nc.scalar.copy)
-        relu(done[n_out][0])
-        store(done[n_out][0])
-        n_out += 1
-        regroup(last, 0, 2, nc.vector.tensor_copy)
+        regroup(last, 0, 4, nc.scalar.copy)
+        regroup(last, 4, 8, nc.scalar.copy)
         quant(ORDER[NG - 2])
         add(done[n_add][0])
         n_add += 1
@@ -283,29 +308,40 @@ def tile_gcnfast_t_kernel(tc, h, e, AA_mask, GCW, GCB, out):
         for s, kk in done[n_mm:]:
             mm_group(s, kk)
         n_mm = len(done)
-        regroup(last, 6, 8, nc.scalar.copy)
-        regroup(last, 4, 6, nc.vector.tensor_copy)
         ends = [(14, slot(13), 0), (15, T15, 1)]
-        banks = {}
+        halves = {}
         for a in range(2):
             quant_part(last, a)
-            while n_add < n_mm - 1 + a:
+            if a == 0:
                 add(done[n_add][0])
                 n_add += 1
             for s, kt, half in ends:
                 move_part(half, k, kt, a)
-                for tr in range(4 * a, 4 * a + 4):
-                    for b in range(4):
-                        if tr == 0:
-                            banks[(s, b)] = psa.tile([P, 512], F32, name="acc", tag="acc")
-                        mm(s, kt, b, tr, banks[(s, b)], 0)
+                halves[(s, a)] = psa.tile([P, 512], F32, name="acc", tag="acc")
+                for b in range(4):
+                    for tr in range(4 * a, 4 * a + 4):
+                        mm(s, kt, b, tr, halves[(s, a)], P * b, 4 * a, 4 * a + 3)
+        while n_add < n_mm:
+            add(done[n_add][0])
+            n_add += 1
         while n_out < n_add:
             relu(done[n_out][0])
             store(done[n_out][0])
             n_out += 1
         for s, kt, half in ends:
             ys[s] = yp.tile([P, 4, P], F32, name="y", tag="y")
-            for b in range(4):
-                nc.vector.tensor_tensor(out=ys[s][:, b, :], in0=banks[(s, b)][:, 0:P], in1=bias[:], op=ALU.add)
+            nc.vector.tensor_tensor(
+                out=ys[s][:],
+                in0=halves[(s, 0)][:].rearrange("p (b d) -> p b d", b=4),
+                in1=bias[:].unsqueeze(1).to_broadcast([P, 4, P]),
+                op=ALU.add,
+            )
+        for s, kt, half in ends:
+            nc.vector.tensor_tensor(
+                out=ys[s][:],
+                in0=halves[(s, 1)][:].rearrange("p (b d) -> p b d", b=4),
+                in1=ys[s][:],
+                op=ALU.add,
+            )
             relu(s)
             store(s)

@@ -61,12 +61,12 @@ def tile_gcnfast_t_kernel(tc, h, e, AA_mask, GCW, GCB, out):
 
         def load(g):
             raw[g] = rawp.tile([P, 4, 8, P], BF16, name="raw", tag="raw")
-            u = g % 2
+            u = 1 - g % 2
             flat = raw[g][:].rearrange("p j t d -> p j (t d)")
             if g == 0:
                 for a in range(2):
                     nc.sync.dma_start(
-                        out=flat[:, :, 512 * a : 512 * a + 512], in_=hv[0, 0:P, :, 512 * a : 512 * a + 512]
+                        out=flat[:, :, 512 * a : 512 * a + 512], in_=hv[u, 0:P, :, 512 * a : 512 * a + 512]
                     )
             elif g == 15:
                 nc.sync.dma_start(out=flat[0:64], in_=hv[u, 960:1024])
@@ -87,7 +87,7 @@ def tile_gcnfast_t_kernel(tc, h, e, AA_mask, GCW, GCB, out):
                 op(out=dst[:, a:b], in_=src[:, a:b])
 
         def v_pieces(g):
-            return 0 if g == ORDER[-1] else 2 + 2 * (g % 2)
+            return 0 if g == ORDER[-1] else 2
 
         def on_tensor(g):
             return g in ORDER[2:14]
@@ -142,7 +142,7 @@ def tile_gcnfast_t_kernel(tc, h, e, AA_mask, GCW, GCB, out):
             nc.vector.tensor_copy(out=cods[p, k_to, :].bitcast(I32), in_=cods[p, k_from, :].bitcast(I32))
 
         def mm(s, k, b, tr, bank, lo, first=0, last=7):
-            par = s % 2
+            par = 1 - s % 2
             nc.tensor.matmul_mx(
                 out=bank[:, lo : lo + P],
                 lhsT=a_codes[:, par, 1024 * b + P * tr : 1024 * b + P * tr + P].bitcast(FP8X4),
@@ -243,18 +243,19 @@ def tile_gcnfast_t_kernel(tc, h, e, AA_mask, GCW, GCB, out):
                     out=a_scl[lo : lo + 4, 1, :].bitcast(I32), in_=a_scl[fr : fr + 4, 0, :].bitcast(I32)
                 )
 
+        for b in range(4):
+            place_weights(0, b)
+        load(ORDER[AHEAD])
+        regroup_v(0)
         nc.vector.memset(a_codes[:, 1, 2048:4096].bitcast(I32), 0)
         nc.vector.memset(cods[:, :, 1024:1280].bitcast(I32), 0)
         place_scales()
         place_weights(1, 0)
         place_weights(1, 1)
-        load(ORDER[AHEAD])
+        load(ORDER[AHEAD + 1])
         place_weights(1, 2)
         place_weights(1, 3)
-        load(ORDER[AHEAD + 1])
-        for b in range(4):
-            place_weights(0, b)
-        regroup_v(0)
+        load(ORDER[AHEAD + 2])
 
         done = []
 
@@ -278,8 +279,8 @@ def tile_gcnfast_t_kernel(tc, h, e, AA_mask, GCW, GCB, out):
         n_add = 0
         n_out = 0
         for j in range(1, NG - 1):
-            if j + AHEAD + 1 < NG:
-                load(ORDER[j + AHEAD + 1])
+            if j + AHEAD + 2 < NG:
+                load(ORDER[j + AHEAD + 2])
             regroup_s(ORDER[j])
             if n_out < n_add - 1:
                 relu(done[n_out][0])
@@ -299,8 +300,9 @@ def tile_gcnfast_t_kernel(tc, h, e, AA_mask, GCW, GCB, out):
 
         last = ORDER[NG - 1]
         k = slot(last)
-        regroup(last, 0, 4, nc.scalar.copy)
-        regroup(last, 4, 8, nc.scalar.copy)
+        regroup(last, 2, 4, nc.scalar.copy)
+        regroup(last, 5, 8, nc.scalar.copy)
+        regroup(last, 0, 2, nc.vector.tensor_copy)
         quant(ORDER[NG - 2])
         add(done[n_add][0])
         n_add += 1
@@ -313,8 +315,7 @@ def tile_gcnfast_t_kernel(tc, h, e, AA_mask, GCW, GCB, out):
         for a in range(2):
             quant_part(last, a)
             if a == 0:
-                add(done[n_add][0])
-                n_add += 1
+                regroup(last, 4, 5, nc.vector.tensor_copy)
             for s, kt, half in ends:
                 move_part(half, k, kt, a)
                 halves[(s, a)] = psa.tile([P, 512], F32, name="acc", tag="acc")

from contextlib import ExitStack

import concourse.mybir as mybir
from concourse.masks import make_identity

BF16 = mybir.dt.bfloat16
F32 = mybir.dt.float32
U32 = mybir.dt.uint32
U8 = mybir.dt.uint8
I32 = mybir.dt.int32
FP8X4 = mybir.dt.float8_e4m3fn_x4
ALU = mybir.AluOpType
ACT = mybir.ActivationFunctionType

P = 128
FLOPS = 2 * 64 * 128 * 1024 * 128
ORDER = list(range(0, 8)) + [15] + list(range(8, 15))
NG = 16
RING = 5
T0, T15, TZ = RING, RING + 1, RING + 2
AHEAD = 5


def tile_gcnfast_t_kernel(tc, h, e, AA_mask, GCW, GCB, out):
    nc = tc.nc
    with ExitStack() as ctx:
        ctx.enter_context(tc.manual_schedule())
        const = ctx.enter_context(tc.tile_pool(name="const", bufs=1))
        rawp = ctx.enter_context(tc.tile_pool(name="rawp", bufs=9))
        grpp = ctx.enter_context(tc.tile_pool(name="grpp", bufs=4))
        yp = ctx.enter_context(tc.tile_pool(name="yp", bufs=7))
        psa = ctx.enter_context(tc.psum_pool(name="psa", bufs=6))
        psr = ctx.enter_context(tc.psum_pool(name="psr", bufs=2))

        hv = h.rearrange("b (c j) (u t) d -> u (b c) j (t d)", j=4, u=2)
        ov = out.rearrange("b s t d -> (s t) b d")

        ident = const.tile([P, P], F32, name="ident")
        perm = const.tile([P, P], F32, name="perm")
        permb = const.tile([P, P], BF16, name="permb")
        identb = const.tile([P, P], BF16, name="identb")
        gcw = const.tile([P, 1024], BF16, name="gcw")
        msk = const.tile([P, 1024], BF16, name="msk")
        pm = const.tile([P, 1024], BF16, name="pm")
        gcb = const.tile([P, P], BF16, name="gcb")
        bias = const.tile([P, P], F32, name="bias")
        warm = const.tile([P, 16], F32, name="warm")
        cd = const.tile([P, 1024], U32, name="cd", align_bytes=64)
        a_scl = const.tile([P, 2, 1024], U8, name="a_scl", align_bytes=64)
        a_codes = const.tile([P, 2, 4096], U32, name="a_codes", align_bytes=64)
        cods = const.tile([P, RING + 3, 1280], U32, name="cods", align_bytes=64)

        raw = {}
        reg = {}
        grp = {}
        acc = {}
        ys = {}

        def slot(g):
            return T0 if g == 0 else T15 if g == 15 else g % RING

        def load(g):
            raw[g] = rawp.tile([P, 4, 8, P], BF16, name="raw", tag="raw")
            u = 1 - g % 2
            flat = raw[g][:].rearrange("p j t d -> p j (t d)")
            if g == 0:
                for a in range(2):
                    nc.sync.dma_start(
                        out=flat[:, :, 512 * a : 512 * a + 512], in_=hv[u, 0:P, :, 512 * a : 512 * a + 512]
                    )
            elif g == 15:
                nc.sync.dma_start(out=flat[0:64], in_=hv[u, 960:1024])
                nc.sync.dma_start(out=flat[64:128], in_=hv[u, 0:64])
            else:
                nc.sync.dma_start(out=flat, in_=hv[u, 64 * g : 64 * g + P])

        def regroup(g, a, b, op):
            if b == a:
                return
            if g not in grp:
                grp[g] = grpp.tile([P, 4096], BF16, name="grp", tag="grp", align_bytes=64)
            src = raw[g][:].rearrange("p j t (c i) -> p t c j i", i=4)
            dst = grp[g][:].rearrange("p (t c i j) -> p t c j i", t=8, c=32, i=4, j=4)
            if b - a == 1:
                op(out=dst[:, a], in_=src[:, a])
            elif b > a:
                op(out=dst[:, a:b], in_=src[:, a:b])

        def v_pieces(g):
            return 0 if g == ORDER[-1] else 2

        def on_tensor(g):
            return g in ORDER[2:14]

        def spread_piece(g):
            bank = psr.tile([P, 512], BF16, name="reg", tag="reg")
            slots = bank[:].rearrange("p (d w e) -> p w d e", d=P, w=2, e=2)
            for w in range(2):
                nc.tensor.matmul(
                    out=slots[:, w],
                    lhsT=identb[:],
                    rhs=raw[g][:, 2 * w : 2 * w + 2, 7, :].rearrange("p e d -> p d e"),
                    start=True,
                    stop=True,
                )
            reg[g] = bank

        def regroup_s(g):
            if on_tensor(g):
                regroup(g, v_pieces(g), 7, nc.scalar.copy)
                nc.scalar.copy(out=grp[g][:, 3584:4096], in_=reg[g][:])
            else:
                regroup(g, v_pieces(g), 8, nc.scalar.copy)

        def regroup_v(g):
            regroup(g, 0, v_pieces(g), nc.vector.tensor_copy)

        def quant(g):
            k = slot(g)
            nc.vector.quantize_mx(
                out=cods[:, k, 0:1024].bitcast(FP8X4), scales=cods[:, k, 1024:1280].bitcast(U8), in_=grp[g][:]
            )

        def quant_part(g, a):
            k = slot(g)
            scl = cods[:, k, 1024:1280].bitcast(U8)
            nc.vector.quantize_mx(
                out=cods[:, k, 512 * a : 512 * a + 512].bitcast(FP8X4),
                scales=scl[:, 512 * a : 512 * a + 512],
                in_=grp[g][:, 2048 * a : 2048 * a + 2048],
            )

        def move_part(half, k_from, k_to, a):
            p = slice(64 * half, 64 * half + 64)
            for lo, w in ((512 * a, 512), (1024 + 128 * a, 128)):
                nc.vector.tensor_copy(
                    out=cods[p, k_to, lo : lo + w].bitcast(I32), in_=cods[p, k_from, lo : lo + w].bitcast(I32)
                )

        def move(half, k_from, k_to):
            p = slice(64 * half, 64 * half + 64)
            nc.vector.tensor_copy(out=cods[p, k_to, :].bitcast(I32), in_=cods[p, k_from, :].bitcast(I32))

        def mm(s, k, b, tr, bank, lo, first=0, last=7):
            par = 1 - s % 2
            nc.tensor.matmul_mx(
                out=bank[:, lo : lo + P],
                lhsT=a_codes[:, par, 1024 * b + P * tr : 1024 * b + P * tr + P].bitcast(FP8X4),
                lhsT_scale=a_scl[:, par, P * tr : P * tr + P],
                rhs=cods[:, k, P * tr : P * tr + P].bitcast(FP8X4),
                rhs_scale=cods[:, k, 1024:1280].bitcast(U8)[:, P * tr : P * tr + P],
                start=(tr == first),
                stop=(tr == last),
            )

        def mm_group(s, k):
            acc[s] = psa.tile([P, 512], F32, name="acc", tag="acc")
            for b in range(4):
                for tr in range(8):
                    mm(s, k, b, tr, acc[s], P * b)

        def add(s):
            ys[s] = yp.tile([P, 4, P], F32, name="y", tag="y")
            nc.vector.tensor_tensor(
                out=ys[s][:],
                in0=acc[s][:].rearrange("p (b d) -> p b d", b=4),
                in1=bias[:].unsqueeze(1).to_broadcast([P, 4, P]),
                op=ALU.add,
            )

        def relu(s):
            yf = ys[s][:].rearrange("p b d -> p (b d)")
            nc.scalar.activation(out=yf, in_=yf, func=ACT.Relu)

        def store(s):
            nc.sync.dma_start(out=ov[:, 4 * s : 4 * s + 4, :], in_=ys[s][:])

        nc.gpsimd.memset(warm[:], 0.0)
        make_identity(nc, ident[:])
        nc.gpsimd.memset(a_scl[:, 1, :].bitcast(I32), 0)
        for a in range(4):
            nc.gpsimd.memset(a_codes[:, 1, 512 * a : 512 * a + 512].bitcast(I32), 0)
        nc.vector.memset(a_codes[:, 0, :].bitcast(I32), 0)
        nc.sync.dma_start(out=gcw[:], in_=GCW)
        nc.sync.dma_start(out=msk[:], in_=AA_mask)
        load(0)
        nc.sync.dma_start(out=gcb[:], in_=GCB)
        for g in ORDER[1:AHEAD]:
            load(g)
        nc.scalar.activation(out=warm[:], in_=warm[:], func=ACT.Relu)
        nc.vector.scalar_tensor_tensor(out=pm[:], in0=gcw[:], scalar=0.0, in1=msk[:], op0=ALU.max, op1=ALU.mult)

        pa = grpp.tile([P, 4096], BF16, name="pa", tag="grp", align_bytes=64)
        gd = grpp.tile([P, 4096], BF16, name="gd", tag="grp", align_bytes=64)
        paw = pa[:].bitcast(F32)
        gdw = gd[:].bitcast(F32)
        pav = paw.rearrange("p (t w u b c) -> p w u t b c", t=8, w=2, u=2, b=4, c=16)
        pmv = pm[:].bitcast(F32).rearrange("p (u t c w) -> p w u t c", u=2, t=8, c=16, w=2)
        for w in range(2):
            for u in range(2):
                dst = pav[:, w, u]
                src = pmv[:, w, u].unsqueeze(2).to_broadcast([P, 8, 4, 16])
                if u == 0:
                    nc.vector.tensor_copy(out=dst, in_=src)
                else:
                    nc.scalar.copy(out=dst, in_=src)
        regroup_s(0)
        nc.vector.tensor_copy(
            out=perm[:].rearrange("p (s t) -> p s t", s=8), in_=ident[:].rearrange("p (t s) -> p s t", s=8)
        )
        nc.vector.tensor_copy(out=permb[:], in_=perm[:])
        nc.vector.tensor_copy(out=identb[:], in_=ident[:])
        banks = []
        for k in range(4):
            bank = psa.tile([P, 2, 2, P], F32, name="at", tag="acc")
            for t in range(2):
                for w in range(2):
                    lo = (2 * k + t) * 256 + w * P
                    nc.tensor.transpose(out=bank[:, t, w, :], in_=paw[:, lo : lo + P], identity=perm[:])
            banks.append(bank)
        bps = psa.tile([P, 512], F32, name="bps", tag="acc")
        nc.tensor.matmul(out=bps[:, 0:P], lhsT=permb[:], rhs=gcb[:], start=True, stop=True)
        for k in range(4):
            dst = gdw[:, 512 * k : 512 * k + 512].rearrange("p (t m w) -> p t m w", t=2, m=P, w=2)
            src = banks[k][:].rearrange("p t w m -> p t m w")
            nc.vector.tensor_copy(out=dst, in_=src)
        nc.vector.quantize_mx(out=cd[:].bitcast(FP8X4), scales=a_scl[:, 0, :], in_=gd[:])
        nc.vector.tensor_copy(out=bias[:], in_=bps[:, 0:P])

        def place_weights(par, b):
            for u in range(2):
                lo = 64 * u + 16 * b
                fr = 64 * (u ^ par) + 16 * (b ^ 1)
                nc.sync.dma_start(
                    out=a_codes[lo : lo + 16, par, 1024 * b : 1024 * b + 1024].bitcast(I32),
                    in_=cd[fr : fr + 16, :].bitcast(I32),
                )

        def place_scales():
            for q in range(4):
                lo, fr = 32 * q, 32 * (q ^ 2)
                nc.sync.dma_start(
                    out=a_scl[lo : lo + 4, 1, :].bitcast(I32), in_=a_scl[fr : fr + 4, 0, :].bitcast(I32)
                )

        for b in range(4):
            place_weights(0, b)
        load(ORDER[AHEAD])
        regroup_v(0)
        nc.vector.memset(a_codes[:, 1, 2048:4096].bitcast(I32), 0)
        nc.vector.memset(cods[:, :, 1024:1280].bitcast(I32), 0)
        place_scales()
        place_weights(1, 0)
        place_weights(1, 1)
        load(ORDER[AHEAD + 1])
        place_weights(1, 2)
        place_weights(1, 3)
        load(ORDER[AHEAD + 2])

        done = []

        def complete(g):
            if g == 1:
                move(1, T0, TZ)
                move(0, slot(1), TZ)
                done.append((1, TZ))
            elif g == 15:
                move(1, T15, T0)
                done.append((0, T0))
            elif g > 1:
                move(0, slot(g), slot(g - 1))
                done.append((g, slot(g - 1)))
                if g == 14:
                    move(1, slot(g), T15)
                    done.append((15, T15))

        spread_piece(ORDER[2])
        n_mm = 0
        n_add = 0
        n_out = 0
        for j in range(1, NG - 1):
            if j + AHEAD + 2 < NG:
                load(ORDER[j + AHEAD + 2])
            regroup_s(ORDER[j])
            if n_out < n_add - 1:
                relu(done[n_out][0])
                store(done[n_out][0])
                n_out += 1
            regroup_v(ORDER[j])
            quant(ORDER[j - 1])
            if n_add < n_mm - 1:
                add(done[n_add][0])
                n_add += 1
            complete(ORDER[j - 1])
            if j + 2 < NG and on_tensor(ORDER[j + 2]):
                spread_piece(ORDER[j + 2])
            for s, k in done[n_mm:]:
                mm_group(s, k)
            n_mm = len(done)

        last = ORDER[NG - 1]
        k = slot(last)
        regroup(last, 2, 4, nc.scalar.copy)
        regroup(last, 5, 8, nc.scalar.copy)
        regroup(last, 0, 2, nc.vector.tensor_copy)
        quant(ORDER[NG - 2])
        add(done[n_add][0])
        n_add += 1
        complete(ORDER[NG - 2])
        for s, kk in done[n_mm:]:
            mm_group(s, kk)
        n_mm = len(done)
        ends = [(14, slot(13), 0), (15, T15, 1)]
        halves = {}
        for a in range(2):
            quant_part(last, a)
            if a == 0:
                regroup(last, 4, 5, nc.vector.tensor_copy)
            for s, kt, half in ends:
                move_part(half, k, kt, a)
                halves[(s, a)] = psa.tile([P, 512], F32, name="acc", tag="acc")
                for b in range(4):
                    for tr in range(4 * a, 4 * a + 4):
                        mm(s, kt, b, tr, halves[(s, a)], P * b, 4 * a, 4 * a + 3)
        while n_add < n_mm:
            add(done[n_add][0])
            n_add += 1
        while n_out < n_add:
            relu(done[n_out][0])
            store(done[n_out][0])
            n_out += 1
        for s, kt, half in ends:
            ys[s] = yp.tile([P, 4, P], F32, name="y", tag="y")
            nc.vector.tensor_tensor(
                out=ys[s][:],
                in0=halves[(s, 0)][:].rearrange("p (b d) -> p b d", b=4),
                in1=bias[:].unsqueeze(1).to_broadcast([P, 4, P]),
                op=ALU.add,
            )
        for s, kt, half in ends:
            nc.vector.tensor_tensor(
                out=ys[s][:],
                in0=halves[(s, 1)][:].rearrange("p (b d) -> p b d", b=4),
                in1=ys[s][:],
                op=ALU.add,
            )
            relu(s)
            store(s)
